import numpy as np
import ml_dtypes


def mxq(x, axis, fmt="e4m3"):
    dtype, down = {"e4m3": (ml_dtypes.float8_e4m3fn, 7), "e5m2": (ml_dtypes.float8_e5m2, 14)}[fmt]
    v = np.moveaxis(np.asarray(x, np.float32).astype(ml_dtypes.bfloat16).astype(np.float64), axis, -1)
    blocks = v.reshape(v.shape[:-1] + (-1, 32))
    amax = np.abs(blocks).max(-1, keepdims=True)
    byte = np.maximum(np.where(amax > 0, np.frexp(amax)[1] - 1 + 127, 0) - down, 1)
    scale = np.exp2(byte - 127.0)
    codes = (blocks / scale).astype(np.float32).astype(dtype).astype(np.float64)
    return np.moveaxis((codes * scale).reshape(v.shape), -1, axis)


WIDE = False


def mx_kscale(k):
    if not WIDE:
        return np.ones(k)
    levels = np.array([18, -18])
    if k % 512:
        return np.exp2(np.random.permutation(np.resize(levels, k // 32))).repeat(32)
    a = np.empty((k // 512, 16))
    for p in range(k // 512):
        a[p, :8] = np.random.permutation(np.resize(levels, 8))
        for g in range(8):
            far = levels[np.abs(levels - a[p, g]) >= 10]
            a[p, g + 8] = far[np.random.randint(len(far))]
    return np.exp2(a.ravel()).repeat(32)


BF16 = ml_dtypes.bfloat16


def bf(x):
    return np.asarray(x, np.float32).astype(BF16)


def f64(x):
    return np.asarray(x).astype(np.float64)


G, D1, D2, D3, K, N = 4, 4, 16, 16, 512, 1024
T = D1 * D2 * D3

EPS = 1e-6


def row_stats(xg):
    m = np.mean(xg, axis=-1)
    v = np.mean(np.square(xg - m[..., None]), axis=-1)
    return m, 1.0 / np.sqrt(v + EPS)


def setup_inputs():
    s = mx_kscale(T)
    t = s / np.min(s)
    c = np.min(s)
    u = mx_kscale(N)
    rows = np.random.standard_normal((G, D1, D2, D3, K))
    rows = rows * (0.5 + 1.5 * np.random.random_sample((G, D1, D2, D3, 1))) + 0.5 * np.random.standard_normal((G, D1, D2, D3, 1))
    x0 = bf(rows.reshape(G * K, D1, D2, D3))
    ln_gamma = bf(1.0 + 0.1 * np.random.standard_normal((G, K)))
    ln_beta = bf(0.1 * np.random.standard_normal((G, K)))
    w0 = bf(np.random.standard_normal((G, N, K)) / np.sqrt(K))
    b = bf(0.1 * np.random.standard_normal((G, N)))
    g = np.random.standard_normal((G, N, T)) * np.exp2(np.random.randint(-6, 1, (G, 1, T)))
    g = bf((g / t * u[None, :, None] * c).reshape(G * N, D1, D2, D3))
    m, r = row_stats(f64(x0).reshape(G, D1, D2, D3, K))
    x = bf((f64(x0).reshape(G, T, K) * t[None, :, None]).reshape(G * K, D1, D2, D3))
    return {"x": x,
            "ln_gamma": ln_gamma,
            "ln_beta": ln_beta,
            "W": bf(f64(w0) / u[None, :, None]),
            "b": b,
            "mu": np.asarray(m, np.float32),
            "rstd": np.asarray(r, np.float32),
            "grad_out": g}


def reference(x, ln_gamma, ln_beta, W, b, mu, rstd, grad_out):
    xg = f64(x).reshape(G, T, K)
    m = f64(mu).reshape(G, T, 1)
    r = f64(rstd).reshape(G, T, 1)
    gam = f64(ln_gamma)[:, None, :]
    xhat = (xg - m) * r
    xn = xhat * gam + f64(ln_beta)[:, None, :]
    dy = f64(grad_out).reshape(G, N, T)
    dxn = mxq(dy, 1, "e5m2").transpose(0, 2, 1) @ mxq(f64(W), 1, "e4m3")
    dW = mxq(dy, 2, "e5m2") @ mxq(xn, 1, "e4m3")
    dxhat = dxn * gam
    c1 = np.mean(dxhat, axis=-1, keepdims=True)
    c2 = np.mean(dxhat * xhat, axis=-1, keepdims=True)
    dx = r * (dxhat - c1 - xhat * c2)
    return dx.reshape(G * K, D1, D2, D3), dW

from contextlib import ExitStack

import concourse.mybir as mybir
from concourse.masks import make_identity

G, T, K, N = 4, 1024, 512, 1024
FLOPS = 2 * 2 * G * T * K * N
BYTES = 2 * (G * T * K + G * N * K + G * N * T + 2 * G * K) + 4 * (2 * G * T + G * T * K + G * N * K)

F32 = mybir.dt.float32
BF16 = mybir.dt.bfloat16
U32 = mybir.dt.uint32
U8 = mybir.dt.uint8
E4 = mybir.dt.float8_e4m3fn_x4
E5 = mybir.dt.float8_e5m2_x4
MULT = mybir.AluOpType.mult
ADD = mybir.AluOpType.add
SUB = mybir.AluOpType.subtract
IDENT = mybir.ActivationFunctionType.Identity

P = 128
TILES = T // P
V_COLS = 96


def tile_groupedlinear_v_kernel(tc, x, ln_gamma, ln_beta, W, b, mu, rstd, grad_out, out_0, out_1):
    nc = tc.nc
    dy_hbm = grad_out.rearrange("(g q p j) a b c -> g q p j (a b c)", g=G, q=2, j=4)
    w_hbm = W.rearrange("g (q p j) k -> g q p j k", q=2, j=4)
    x_hbm = x.rearrange("(g k) a b c -> g (k a b c)", g=G).rearrange("g (h i p k) -> g h p i k", h=2, i=4, p=P)
    o0_hbm = out_0.rearrange("(g k) a b c -> g (k a b c)", g=G).rearrange("g (s i p k) -> g s p i k", s=4, i=2, p=P)
    o1_hbm = out_1.rearrange("g (q p j) k -> g q p j k", q=2, j=4)

    with ExitStack() as ctx:
        keep = ctx.enter_context(tc.tile_pool(name="keep", bufs=1))
        raw = ctx.enter_context(tc.tile_pool(name="raw", bufs=4))
        grp = ctx.enter_context(tc.tile_pool(name="grp", bufs=3))
        codes = ctx.enter_context(tc.tile_pool(name="codes", bufs=8))
        work = ctx.enter_context(tc.tile_pool(name="work", bufs=3))
        outs = ctx.enter_context(tc.tile_pool(name="outs", bufs=3))
        ps_tr = ctx.enter_context(tc.psum_pool(name="ps_tr", bufs=4))
        ps_mm = ctx.enter_context(tc.psum_pool(name="ps_mm", bufs=4))

        ident = keep.tile([P, P], F32, name="ident")
        ident_b = keep.tile([P, P], BF16, name="ident_b")
        make_identity(nc, ident[:])
        make_identity(nc, ident_b[:])
        mr_rows = keep.tile([P, P], F32, name="mr_rows")
        gb_rows = keep.tile([P, P], BF16, name="gb_rows")
        gam_rows = keep.tile([P, K], BF16, name="gam_rows")
        mr = keep.tile([P, 64], F32, name="mr")
        nr = keep.tile([P, 32], F32, name="nr")
        gb = keep.tile([P, 32], F32, name="gb")
        gam = keep.tile([P, G, K], BF16, name="gam")

        dy_raw, w_raw, x_raw, xh = {}, {}, {}, {}
        grouped = {}
        q8 = {}
        xnt = {}
        bank = {}
        pmm = {}
        st, dd, xp = {}, {}, {}
        o0, o1 = {}, {}

        def load_dy(g, q, halves=False):
            t = raw.tile([P, 4, T], BF16, name="dy_raw", bufs=4)
            dy_raw[g, q] = t
            if not halves:
                nc.sync.dma_start(out=t[:], in_=dy_hbm[g, q])

        def load_dy_half(g, q, h):
            cols = slice(512 * h, 512 * h + 512)
            nc.sync.dma_start(out=dy_raw[g, q][:, :, cols], in_=dy_hbm[g, q][:, :, cols])

        def load_w(g, q):
            t = raw.tile([P, 4, K], BF16, name="w_raw", bufs=4)
            w_raw[g, q] = t
            nc.sync.dma_start(out=t[:], in_=w_hbm[g, q])

        def load_x(g, h):
            t = raw.tile([P, 4, K], BF16, name="x_raw", bufs=3)
            x_raw[g, h] = t
            nc.sync.dma_start(out=t[:], in_=x_hbm[g, h])

        def interleave(key, v_cols):
            kind, g, q, h = key
            src = w_raw[g, q][:] if kind == "w" else dy_raw[g, q][:, :, 512 * h:512 * h + 512]
            t = grp.tile([P, 512, 4], BF16, name="grp_o", bufs=4, align_bytes=64)
            grouped[key] = t
            s = src.rearrange("p j (c i) -> p c j i", i=4)
            d = t[:].rearrange("p (c i) j -> p c j i", i=4)
            m = v_cols // 4
            if m > 0:
                nc.vector.tensor_copy(out=d[:, :m], in_=s[:, :m])
            if m < 128:
                nc.scalar.copy(out=d[:, m:], in_=s[:, m:])

        def quantize(key, dtype, tag, bufs):
            c = codes.tile([P, 512], U32, name=tag + "_c", bufs=bufs, align_bytes=64)
            s = codes.tile([P, 512], U8, name=tag + "_s", bufs=bufs, align_bytes=64)
            q8[key] = (c, s)
            nc.vector.quantize_mx(out=c[:].bitcast(dtype), scales=s[:], in_=grouped[key][:].rearrange("p c j -> p (c j)"))

        def xhat(g, i):
            h, ii = divmod(i, 4)
            if ii == 0:
                t = work.tile([P, 4, K], F32, name="xh", bufs=3)
                xh[g, h] = t
            col = 8 * g + i
            nc.vector.tensor_scalar(out=xh[g, h][:, ii], in0=x_raw[g, h][:, ii], scalar1=mr[:, col:col + 1],
                                    scalar2=mr[:, 32 + col:33 + col], op0=SUB, op1=MULT)

        def xhat_t(g, h, kb):
            t = ps_tr.tile([P, 4, P], F32, name="tr")
            bank["x", g, h, kb] = t
            for i in range(4):
                nc.tensor.transpose(t[:, i], xh[g, h][:, i, P * kb:P * kb + P], ident[:])

        def affine(g, h, kb):
            t = work.tile([P, 512], BF16, name="xnt", bufs=6, align_bytes=64)
            xnt[g, h, kb] = t
            col = 4 * g + kb
            nc.scalar.activation(out=t[:].rearrange("k (u p e) -> k u p e", u=2, e=2),
                                 in_=bank["x", g, h, kb][:].rearrange("k i m -> k (i m)").rearrange("k (p u e) -> k u p e", u=2, e=2),
                                 func=IDENT, scale=gb[:, col:col + 1], bias=gb[:, 16 + col:17 + col])

        def xn_t(g, h, half):
            t = ps_tr.tile([P, 2, 256], F32, name="tr")
            bank["n", g, h, half] = t
            for k2 in range(2):
                words = xnt[g, h, 2 * half + k2][:].bitcast(F32)
                for u in range(2):
                    nc.tensor.transpose(t[:, u, P * k2:P * k2 + P], words[:, P * u:P * u + P], ident[:])

        def dy_t(g, h, q, half):
            t = ps_tr.tile([P, 2, 256], F32, name="tr")
            bank["y", g, h, q, half] = t
            words = dy_raw[g, q][:].rearrange("p j t -> p (j t)").bitcast(F32)
            for j2 in range(2):
                base = 512 * (2 * half + j2) + 256 * h
                for u in range(2):
                    nc.tensor.transpose(t[:, u, P * j2:P * j2 + P], words[:, base + u:base + 256:2], ident[:])

        def words_out(bkey, gkey, half):
            if half == 0:
                t = grp.tile([P, 512, 4], BF16, name="grp_t", bufs=4, align_bytes=64)
                grouped[gkey] = t
            d = grouped[gkey][:].rearrange("p c j -> p (c j)").bitcast(F32).rearrange("p (c u) -> p c u", u=2)
            nc.scalar.copy(out=d[:, 256 * half:256 * half + 256], in_=bank[bkey][:].rearrange("p u c -> p c u"))

        def mm(key, pairs):
            t = ps_mm.tile([P, 512], F32, name="mm")
            pmm[key] = t
            for n, (lk, col, rk, ldt, rdt) in enumerate(pairs):
                lc, ls = q8[lk]
                rc, rs = q8[rk]
                nc.tensor.matmul_mx(out=t[:], lhsT=lc[:, col:col + P].bitcast(ldt), lhsT_scale=ls[:, col:col + P],
                                    rhs=rc[:].bitcast(rdt), rhs_scale=rs[:], start=(n == 0), stop=(n == len(pairs) - 1))

        def mm_dx(g, i):
            mm(("dx", g, i), [(("y", g, q, i // 4), P * (i % 4), ("w", g, q, 0), E5, E4) for q in range(2)])

        def mm_dw(g, i):
            q, j = divmod(i, 4)
            mm(("dw", g, i), [(("t", g, h, q), P * j, ("n", g, h, 0), E5, E4) for h in range(2)])

        def dw_out(g, i, engine):
            q, j = divmod(i, 4)
            if j % 2 == 0:
                t = outs.tile([P, 2, K], F32, name="o1", bufs=3)
                o1[g, i // 2] = t
            t = o1[g, i // 2]
            if engine == "s":
                nc.scalar.copy(out=t[:, j % 2], in_=pmm["dw", g, i][:])
            else:
                nc.vector.tensor_copy(out=t[:, j % 2], in_=pmm["dw", g, i][:])
            if j % 2 == 1:
                nc.sync.dma_start(out=o1_hbm[g, q][:, j - 1:j + 1], in_=t[:])

        def p1(g, i):
            s = work.tile([P, 2], F32, name="st", bufs=4)
            d = work.tile([P, K], F32, name="dd", bufs=4)
            st[g, i], dd[g, i] = s, d
            col = 8 * g + i
            nc.vector.scalar_tensor_tensor(out=d[:], in0=pmm["dx", g, i][:], scalar=nr[:, col:col + 1], in1=gam[:, g],
                                           op0=MULT, op1=MULT, accum_out=s[:, 0:1])

        def p2(g, i):
            junk = work.tile([P, K], F32, name="junk", bufs=2)
            nc.vector.scalar_tensor_tensor(out=junk[:], in0=dd[g, i][:], scalar=1.0, in1=xh[g, i // 4][:, i % 4],
                                           op0=MULT, op1=MULT, accum_out=st[g, i][:, 1:2])

        def xprime(g, i):
            t = work.tile([P, K], F32, name="xp", bufs=3)
            xp[g, i] = t
            nc.gpsimd.tensor_scalar(out=t[:], in0=xh[g, i // 4][:, i % 4], scalar1=st[g, i][:, 1:2],
                                    scalar2=st[g, i][:, 0:1], op0=MULT, op1=ADD)

        def p3(g, i):
            if i % 2 == 0:
                t = outs.tile([P, 2, K], F32, name="o0", bufs=3)
                o0[g, i // 2] = t
            t = o0[g, i // 2]
            nc.vector.scalar_tensor_tensor(out=t[:, i % 2], in0=dd[g, i][:], scalar=-float(K), in1=xp[g, i][:],
                                           op0=MULT, op1=ADD)
            if i % 2 == 1:
                nc.sync.dma_start(out=o0_hbm[g, i // 2], in_=t[:])

        with tc.manual_schedule():
            load_dy(0, 0, True)
            load_dy(0, 1, True)
            load_dy_half(0, 0, 0)
            load_w(0, 0)
            load_dy_half(0, 1, 0)
            load_w(0, 1)
            load_x(0, 0)
            load_dy_half(0, 0, 1)
            load_dy_half(0, 1, 1)
            load_x(0, 1)
            load_w(1, 0)
            load_w(1, 1)
            load_dy(1, 0)
            load_dy(1, 1)
            load_x(1, 0)
            nc.vector.memset(mr_rows[:], 0.0)
            nc.vector.memset(gb_rows[:], 0.0)
            nc.vector.memset(gam_rows[:], 0.0)
            warm = keep.tile([P, 1], F32, name="warm")
            nc.vector.memset(warm[:], 0.0)
            nc.scalar.activation(out=warm[:], in_=warm[:], func=IDENT)
            nc.scalar.dma_start(out=mr_rows[0:32, :], in_=mu.rearrange("g a (b0 b1) c -> (g a b0) (b1 c)", b1=8))
            nc.scalar.dma_start(out=mr_rows[32:64, :], in_=rstd.rearrange("g a (b0 b1) c -> (g a b0) (b1 c)", b1=8))
            nc.scalar.dma_start(out=gb_rows[0:16, :], in_=ln_gamma.rearrange("g (kb c) -> (g kb) c", c=P))
            nc.scalar.dma_start(out=gb_rows[16:32, :], in_=ln_beta.rearrange("g (kb c) -> (g kb) c", c=P))
            nc.scalar.dma_start(out=gam_rows[0:4, :], in_=ln_gamma)

            t_mr = ps_tr.tile([P, P], F32, name="tr")
            nc.tensor.transpose(t_mr[:], mr_rows[:], ident[:])
            t_gb = ps_tr.tile([P, P], BF16, name="tr")
            nc.tensor.transpose(t_gb[:], gb_rows[:], ident_b[:])
            nc.vector.tensor_copy(out=mr[:], in_=t_mr[:, 0:64])
            nc.vector.tensor_copy(out=gb[:], in_=t_gb[:, 0:32])
            nc.vector.tensor_scalar(out=nr[:], in0=mr[:, 32:64], scalar1=-1.0 / K, scalar2=None, op0=MULT)
            for g in range(G):
                t = ps_mm.tile([P, K], F32, name="mm")
                nc.tensor.matmul(t[:], lhsT=ident_b[:, g:g + 1].to_broadcast([P, P]), rhs=gam_rows[:], start=True, stop=True)
                nc.scalar.copy(out=gam[:, g], in_=t[:])

            def prep(key, v_cols=V_COLS):
                interleave(key, v_cols)

            def prep_q(key):
                if key[0] == "w":
                    quantize(key, E4, "wq", 4)
                else:
                    quantize(key, E5, "yq", 6)

            first = [("y", 0, 0, 0), ("w", 0, 0, 0), ("y", 0, 1, 0), ("w", 0, 1, 0)]
            for n, key in enumerate(first):
                prep(key, 256)
                if n > 0:
                    prep_q(first[n - 1])
            prep_q(first[3])
            for i in range(4):
                xhat(0, i)
            mm_dx(0, 0)
            mm_dx(0, 1)
            p1(0, 0)

            last = 8 * G
            units = []
            for g in range(1, G):
                units += [None, [("w", g, 0, 0)], [("w", g, 1, 0)], [("y", g, 0, 0)], [("y", g, 1, 0)], None,
                          [("y", g, 0, 1)], [("y", g, 1, 1)]]
            units[0] = [("y", 0, 0, 1), ("y", 0, 1, 1)]
            for tau in range(last + 12):
                g, s = divmod(tau, 8)
                live = tau < last
                if g + 2 < G and s == 5:
                    load_w(g + 2, 0)
                    load_w(g + 2, 1)
                if g + 2 < G and s == 6:
                    load_dy(g + 2, 0)
                if 0 < g and g + 1 < G and s == 0:
                    load_dy(g + 1, 1)
                    load_x(g + 1, 0)
                if g + 1 < G and s == 4:
                    load_x(g + 1, 1)
                if live:
                    h, r = divmod(s, 4)
                    xhat_t(g, h, r)
                    dy_t(g, h, r // 2, r % 2)
                for lag, half in ((2, 0), (4, 1)):
                    if tau - lag >= 0 and (tau - lag) % 4 == 0 and tau - lag < last:
                        gg, ss = divmod(tau - lag, 8)
                        xn_t(gg, ss // 4, half)
                if tau + 2 < last:
                    mm_dx(*divmod(tau + 2, 8))
                if 0 <= tau - 10 < last:
                    mm_dw(*divmod(tau - 10, 8))
                if live:
                    affine(g, h, r)
                    words_out(("y", g, h, r // 2, r % 2), ("t", g, h, r // 2), r % 2)
                for lag, half in ((2, 0), (4, 1)):
                    if tau - lag >= 0 and (tau - lag) % 4 == 0 and tau - lag < last:
                        gg, ss = divmod(tau - lag, 8)
                        words_out(("n", gg, ss // 4, half), ("n", gg, ss // 4, 0), half)
                if 0 <= tau - 11 < last:
                    gg, ii = divmod(tau - 11, 8)
                    dw_out(gg, ii, "v" if (tau > last + 2 and ii % 2 == 0) else "s")
                if live:
                    p2(g, s)
                    xprime(g, s)
                if tau + 1 < last:
                    p1(*divmod(tau + 1, 8))
                if tau < len(units) and units[tau] is not None:
                    for key in units[tau]:
                        prep(key)
                if 0 < tau <= len(units) and units[tau - 1] is not None:
                    for key in units[tau - 1]:
                        prep_q(key)
                if tau >= 2 and (tau - 2) % 2 == 0 and tau - 2 < last:
                    gg, ss = divmod(tau - 2, 8)
                    quantize(("t", gg, ss // 4, (ss % 4) // 2), E5, "tq", 8)
                if tau >= 5 and (tau - 5) % 4 == 0 and tau - 5 < last:
                    gg, ss = divmod(tau - 5, 8)
                    quantize(("n", gg, ss // 4, 0), E4, "nq", 4)
                if tau + 4 < last:
                    xhat(*divmod(tau + 4, 8))
                if live:
                    p3(g, s)
